import numpy as np
import ml_dtypes


def mxq(x, axis, fmt="e4m3"):
    dtype, down = {"e4m3": (ml_dtypes.float8_e4m3fn, 7), "e5m2": (ml_dtypes.float8_e5m2, 14)}[fmt]
    v = np.moveaxis(np.asarray(x, np.float32).astype(ml_dtypes.bfloat16).astype(np.float64), axis, -1)
    blocks = v.reshape(v.shape[:-1] + (-1, 32))
    amax = np.abs(blocks).max(-1, keepdims=True)
    byte = np.maximum(np.where(amax > 0, np.frexp(amax)[1] - 1 + 127, 0) - down, 1)
    scale = np.exp2(byte - 127.0)
    codes = (blocks / scale).astype(np.float32).astype(dtype).astype(np.float64)
    return np.moveaxis((codes * scale).reshape(v.shape), -1, axis)


WIDE = False


def mx_kscale(k):
    if not WIDE:
        return np.ones(k)
    levels = np.array([10, -10, 5, -5, 0])
    a = np.random.permutation(np.resize(levels, k // 512 * 4)).reshape(k // 512, 4)
    idx = np.arange(k)
    return np.exp2(a[idx // 512, idx % 128 // 32])


BF16 = ml_dtypes.bfloat16


def bf(x):
    return np.asarray(x, np.float32).astype(BF16)


def f64(x):
    return np.asarray(x).astype(np.float64)


B, NQ = 256, 12
CONTROL = 0
DIM = 1 << NQ
HALF = DIM // 2


def setup_inputs():
    on = np.nonzero((np.arange(DIM) & (1 << (NQ - CONTROL - 1))) != 0)[0]
    sv = np.ones(DIM)
    sv[on] = mx_kscale(HALF)
    return {"state": bf(np.random.standard_normal((B, DIM)) * sv),
            "target_matrix": bf(np.random.standard_normal((DIM, DIM)) / np.sqrt(HALF) / sv[:, None]),
            "control": CONTROL,
            "num_qubits": NQ}


def reference(state, target_matrix, control, num_qubits):
    dim = 1 << num_qubits
    mask = 1 << (num_qubits - control - 1)
    c1_mask = (np.arange(dim) & mask) != 0
    on = np.nonzero(c1_mask)[0]
    st, tm = f64(state), f64(target_matrix)
    transformed = mxq(st[:, on], 1, "e4m3") @ mxq(tm[np.ix_(on, on)], 0, "e4m3")
    out = st.copy()
    out[:, on] = transformed
    return out

@@ -1,0 +1,132 @@
+from contextlib import ExitStack
+
+import concourse.mybir as mybir
+from concourse.masks import make_identity
+
+BF16 = mybir.dt.bfloat16
+F32 = mybir.dt.float32
+U32 = mybir.dt.uint32
+U8 = mybir.dt.uint8
+FP8X4 = mybir.dt.float8_e4m3fn_x4
+
+P = 128
+PACK = 4
+K_PASS = P * PACK
+BATCH = 256
+DIM = 4096
+HALF = DIM // 2
+ROW_TILES = BATCH // P
+PASSES = HALF // K_PASS
+N_TILE = 512
+COL_TILES = HALF // N_TILE
+PSUM_BANKS = 8
+RUN = 4
+GROUPED_BUFS = 6
+
+FLOPS = 2 * BATCH * HALF * HALF
+BYTES = 2 * BATCH * DIM + 2 * HALF * HALF + 4 * BATCH * DIM
+
+
+def copy_on(nc, on_scalar, out, in_):
+    if on_scalar:
+        nc.scalar.copy(out=out, in_=in_)
+    else:
+        nc.vector.tensor_copy(out=out, in_=in_)
+
+
+def tile_builtcontrolled_kernel(tc, state, target_matrix, control, num_qubits, out):
+    nc = tc.nc
+    assert control == 0 and num_qubits == 12
+
+    with ExitStack() as pools:
+        keep = pools.enter_context(tc.tile_pool(name="keep", bufs=1))
+        stage = pools.enter_context(tc.tile_pool(name="stage", bufs=GROUPED_BUFS))
+        psum = pools.enter_context(tc.psum_pool(name="psum", bufs=PSUM_BANKS))
+
+        x_rows = []
+        for m in range(ROW_TILES):
+            x_tile = keep.tile([P, DIM], BF16, name="x_rows%d" % m)
+            nc.sync.dma_start(out=x_tile[:], in_=state[m * P : (m + 1) * P, :])
+            x_rows.append(x_tile)
+        w_raw = []
+        for c in range(PASSES):
+            w_tile = keep.tile([P, PACK, HALF], BF16, name="w_raw%d" % c)
+            k_rows = target_matrix[HALF + c * K_PASS : HALF + (c + 1) * K_PASS, HALF:DIM]
+            nc.sync.dma_start(out=w_tile[:], in_=k_rows.rearrange("(p t) n -> p t n", t=PACK))
+            w_raw.append(w_tile)
+
+        ident = keep.tile([P, P], F32, name="ident")
+        make_identity(nc, ident[:])
+
+        x_codes = []
+        x_scales = []
+        for m in range(ROW_TILES):
+            pairs = x_rows[m][:].bitcast(F32).rearrange("r (g p u) -> r g u p", p=P, u=2)
+            x_grouped = keep.tile([P, PASSES * P * PACK], BF16, name="x_grouped%d" % m, align_bytes=64)
+            grouped_pairs = x_grouped[:].bitcast(F32).rearrange("p (c r u) -> p c r u", r=P, u=2)
+            for half in range(2):
+                flipped = psum.tile([P, 2, 2, P], F32, name="flipped", tag="bank")
+                for a in range(2):
+                    c = 2 * half + a
+                    for u in range(2):
+                        nc.tensor.transpose(flipped[:, a, u, :], pairs[:, PASSES + c, u, :], ident[:])
+                copy_on(
+                    nc,
+                    half == 1,
+                    grouped_pairs[:, 2 * half : 2 * half + 2, :, :],
+                    flipped[:].rearrange("p a u r -> p a r u"),
+                )
+            codes = keep.tile([P, PASSES * P], U32, name="x_codes%d" % m, align_bytes=64)
+            scales = keep.tile([P, PASSES * P], U8, name="x_scales%d" % m, align_bytes=64)
+            nc.vector.quantize_mx(out=codes[:].bitcast(FP8X4), scales=scales[:], in_=x_grouped[:])
+            x_codes.append(codes)
+            x_scales.append(scales)
+
+        for m in range(ROW_TILES):
+            kept = keep.tile([P, HALF], F32, name="kept%d" % m)
+            copy_on(nc, m == 0, kept[:], x_rows[m][:, 0:HALF])
+            nc.sync.dma_start(out=out[m * P : (m + 1) * P, 0:HALF], in_=kept[:])
+
+        acc = [
+            [psum.tile([P, N_TILE], F32, name="acc_%d_%d" % (m, n), tag="bank") for n in range(COL_TILES)]
+            for m in range(ROW_TILES)
+        ]
+        for c in range(PASSES):
+            w_codes = keep.tile([P, HALF], U32, name="w_codes%d" % c, align_bytes=64)
+            w_scales = keep.tile([P, HALF], U8, name="w_scales%d" % c, align_bytes=64)
+            w_grouped = []
+            for n in range(COL_TILES):
+                grouped = stage.tile([P, N_TILE, PACK], BF16, name="w_grouped", align_bytes=64)
+                copy_on(
+                    nc,
+                    n % 2 == 1,
+                    grouped[:].rearrange("p (g i) t -> p g t i", i=RUN),
+                    w_raw[c][:, :, n * N_TILE : (n + 1) * N_TILE].rearrange("p t (g i) -> p g t i", i=RUN),
+                )
+                w_grouped.append(grouped)
+            for n in range(COL_TILES):
+                cols = slice(n * N_TILE, (n + 1) * N_TILE)
+                nc.vector.quantize_mx(
+                    out=w_codes[:, cols].bitcast(FP8X4),
+                    scales=w_scales[:, cols],
+                    in_=w_grouped[n][:].rearrange("p n t -> p (n t)"),
+                )
+                for m in range(ROW_TILES):
+                    nc.tensor.matmul_mx(
+                        out=acc[m][n][:],
+                        lhsT=x_codes[m][:, c * P : (c + 1) * P].bitcast(FP8X4),
+                        lhsT_scale=x_scales[m][:, c * P : (c + 1) * P],
+                        rhs=w_codes[:, cols].bitcast(FP8X4),
+                        rhs_scale=w_scales[:, cols],
+                        start=(c == 0),
+                        stop=(c == PASSES - 1),
+                    )
+
+        for n in range(COL_TILES):
+            for m in range(ROW_TILES):
+                product = keep.tile([P, N_TILE], F32, name="product_%d_%d" % (m, n))
+                copy_on(nc, m == 1, product[:], acc[m][n][:])
+                nc.sync.dma_start(
+                    out=out[m * P : (m + 1) * P, HALF + n * N_TILE : HALF + (n + 1) * N_TILE],
+                    in_=product[:],
+                )

@@ -52,7 +52,14 @@ def tile_builtcontrolled_kernel(tc, state, target_matrix, control, num_qubits, o
         for c in range(PASSES):
             w_tile = keep.tile([P, PACK, HALF], BF16, name="w_raw%d" % c)
             k_rows = target_matrix[HALF + c * K_PASS : HALF + (c + 1) * K_PASS, HALF:DIM]
-            nc.sync.dma_start(out=w_tile[:], in_=k_rows.rearrange("(p t) n -> p t n", t=PACK))
+            by_partition = k_rows.rearrange("(p t) n -> p t n", t=PACK)
+            pieces = 2 if c in (0, PASSES - 1) else 1
+            width = HALF // pieces
+            for i in range(pieces):
+                nc.sync.dma_start(
+                    out=w_tile[:, :, i * width : (i + 1) * width],
+                    in_=by_partition[:, :, i * width : (i + 1) * width],
+                )
             w_raw.append(w_tile)
 
         ident = keep.tile([P, P], F32, name="ident")
@@ -91,36 +98,50 @@ def tile_builtcontrolled_kernel(tc, state, target_matrix, control, num_qubits, o
             [psum.tile([P, N_TILE], F32, name="acc_%d_%d" % (m, n), tag="bank") for n in range(COL_TILES)]
             for m in range(ROW_TILES)
         ]
+        w_codes = []
+        w_scales = []
         for c in range(PASSES):
-            w_codes = keep.tile([P, HALF], U32, name="w_codes%d" % c, align_bytes=64)
-            w_scales = keep.tile([P, HALF], U8, name="w_scales%d" % c, align_bytes=64)
-            w_grouped = []
-            for n in range(COL_TILES):
-                grouped = stage.tile([P, N_TILE, PACK], BF16, name="w_grouped", align_bytes=64)
-                copy_on(
-                    nc,
-                    n % 2 == 1,
-                    grouped[:].rearrange("p (g i) t -> p g t i", i=RUN),
-                    w_raw[c][:, :, n * N_TILE : (n + 1) * N_TILE].rearrange("p t (g i) -> p g t i", i=RUN),
+            w_codes.append(keep.tile([P, HALF], U32, name="w_codes%d" % c, align_bytes=64))
+            w_scales.append(keep.tile([P, HALF], U8, name="w_scales%d" % c, align_bytes=64))
+
+        def regroup(c, n, on_scalar):
+            grouped = stage.tile([P, N_TILE, PACK], BF16, name="w_grouped", align_bytes=64)
+            copy_on(
+                nc,
+                on_scalar,
+                grouped[:].rearrange("p (g i) t -> p g t i", i=RUN),
+                w_raw[c][:, :, n * N_TILE : (n + 1) * N_TILE].rearrange("p t (g i) -> p g t i", i=RUN),
+            )
+            return grouped
+
+        def quantise_and_multiply(c, n, grouped):
+            cols = slice(n * N_TILE, (n + 1) * N_TILE)
+            nc.vector.quantize_mx(
+                out=w_codes[c][:, cols].bitcast(FP8X4),
+                scales=w_scales[c][:, cols],
+                in_=grouped[:].rearrange("p n t -> p (n t)"),
+            )
+            for m in range(ROW_TILES):
+                nc.tensor.matmul_mx(
+                    out=acc[m][n][:],
+                    lhsT=x_codes[m][:, c * P : (c + 1) * P].bitcast(FP8X4),
+                    lhsT_scale=x_scales[m][:, c * P : (c + 1) * P],
+                    rhs=w_codes[c][:, cols].bitcast(FP8X4),
+                    rhs_scale=w_scales[c][:, cols],
+                    start=(c == 0),
+                    stop=(c == PASSES - 1),
                 )
-                w_grouped.append(grouped)
-            for n in range(COL_TILES):
-                cols = slice(n * N_TILE, (n + 1) * N_TILE)
-                nc.vector.quantize_mx(
-                    out=w_codes[:, cols].bitcast(FP8X4),
-                    scales=w_scales[:, cols],
-                    in_=w_grouped[n][:].rearrange("p n t -> p (n t)"),
-                )
-                for m in range(ROW_TILES):
-                    nc.tensor.matmul_mx(
-                        out=acc[m][n][:],
-                        lhsT=x_codes[m][:, c * P : (c + 1) * P].bitcast(FP8X4),
-                        lhsT_scale=x_scales[m][:, c * P : (c + 1) * P],
-                        rhs=w_codes[:, cols].bitcast(FP8X4),
-                        rhs_scale=w_scales[:, cols],
-                        start=(c == 0),
-                        stop=(c == PASSES - 1),
-                    )
+
+        late = None
+        for c in range(PASSES):
+            for pair in range(COL_TILES // 2):
+                by_vector = regroup(c, 2 * pair, False)
+                by_scalar = regroup(c, 2 * pair + 1, True)
+                if late is not None:
+                    quantise_and_multiply(late[0], late[1], late[2])
+                quantise_and_multiply(c, 2 * pair, by_vector)
+                late = (c, 2 * pair + 1, by_scalar)
+        quantise_and_multiply(late[0], late[1], late[2])
 
         for n in range(COL_TILES):
             for m in range(ROW_TILES):

@@ -19,6 +19,9 @@ ROW_TILES = BATCH // P
 PASSES = HALF // K_PASS
 N_TILE = 512
 COL_TILES = HALF // N_TILE
+SIDES = 2
+SIDE_COLS = HALF // SIDES
+SIDE_TILES = COL_TILES // SIDES
 PSUM_BANKS = 8
 RUN = 4
 GROUPED_BUFS = 6
@@ -49,18 +52,16 @@ def tile_builtcontrolled_kernel(tc, state, target_matrix, control, num_qubits, o
             nc.sync.dma_start(out=x_tile[:], in_=state[m * P : (m + 1) * P, :])
             x_rows.append(x_tile)
         w_raw = []
-        for c in range(PASSES):
-            w_tile = keep.tile([P, PACK, HALF], BF16, name="w_raw%d" % c)
-            k_rows = target_matrix[HALF + c * K_PASS : HALF + (c + 1) * K_PASS, HALF:DIM]
-            by_partition = k_rows.rearrange("(p t) n -> p t n", t=PACK)
-            pieces = 2 if c in (0, PASSES - 1) else 1
-            width = HALF // pieces
-            for i in range(pieces):
-                nc.sync.dma_start(
-                    out=w_tile[:, :, i * width : (i + 1) * width],
-                    in_=by_partition[:, :, i * width : (i + 1) * width],
-                )
-            w_raw.append(w_tile)
+        for side in range(SIDES):
+            w_raw.append([])
+            for c in range(PASSES):
+                w_tile = keep.tile([P, PACK, SIDE_COLS], BF16, name="w_raw_%d_%d" % (side, c))
+                first_col = HALF + side * SIDE_COLS
+                k_rows = target_matrix[
+                    HALF + c * K_PASS : HALF + (c + 1) * K_PASS, first_col : first_col + SIDE_COLS
+                ]
+                nc.sync.dma_start(out=w_tile[:], in_=k_rows.rearrange("(p t) n -> p t n", t=PACK))
+                w_raw[side].append(w_tile)
 
         ident = keep.tile([P, P], F32, name="ident")
         make_identity(nc, ident[:])
@@ -110,7 +111,9 @@ def tile_builtcontrolled_kernel(tc, state, target_matrix, control, num_qubits, o
                 nc,
                 on_scalar,
                 grouped[:].rearrange("p (g i) t -> p g t i", i=RUN),
-                w_raw[c][:, :, n * N_TILE : (n + 1) * N_TILE].rearrange("p t (g i) -> p g t i", i=RUN),
+                w_raw[n // SIDE_TILES][c][
+                    :, :, (n % SIDE_TILES) * N_TILE : (n % SIDE_TILES + 1) * N_TILE
+                ].rearrange("p t (g i) -> p g t i", i=RUN),
             )
             return grouped
 
@@ -132,22 +135,26 @@ def tile_builtcontrolled_kernel(tc, state, target_matrix, control, num_qubits, o
                     stop=(c == PASSES - 1),
                 )
 
+        def store_side(side):
+            for n in range(side * SIDE_TILES, (side + 1) * SIDE_TILES):
+                for m in range(ROW_TILES):
+                    product = keep.tile([P, N_TILE], F32, name="product_%d_%d" % (m, n))
+                    copy_on(nc, m == 1, product[:], acc[m][n][:])
+                    nc.sync.dma_start(
+                        out=out[m * P : (m + 1) * P, HALF + n * N_TILE : HALF + (n + 1) * N_TILE],
+                        in_=product[:],
+                    )
+
         late = None
-        for c in range(PASSES):
-            for pair in range(COL_TILES // 2):
-                by_vector = regroup(c, 2 * pair, False)
-                by_scalar = regroup(c, 2 * pair + 1, True)
+        for side in range(SIDES):
+            for c in range(PASSES):
+                by_vector = regroup(c, side * SIDE_TILES, False)
+                by_scalar = regroup(c, side * SIDE_TILES + 1, True)
+                if side > 0 and c == 1:
+                    store_side(side - 1)
                 if late is not None:
                     quantise_and_multiply(late[0], late[1], late[2])
-                quantise_and_multiply(c, 2 * pair, by_vector)
-                late = (c, 2 * pair + 1, by_scalar)
+                quantise_and_multiply(c, side * SIDE_TILES, by_vector)
+                late = (c, side * SIDE_TILES + 1, by_scalar)
         quantise_and_multiply(late[0], late[1], late[2])
-
-        for n in range(COL_TILES):
-            for m in range(ROW_TILES):
-                product = keep.tile([P, N_TILE], F32, name="product_%d_%d" % (m, n))
-                copy_on(nc, m == 1, product[:], acc[m][n][:])
-                nc.sync.dma_start(
-                    out=out[m * P : (m + 1) * P, HALF + n * N_TILE : HALF + (n + 1) * N_TILE],
-                    in_=product[:],
-                )
+        store_side(SIDES - 1)

@@ -145,16 +145,10 @@ def tile_builtcontrolled_kernel(tc, state, target_matrix, control, num_qubits, o
                         in_=product[:],
                     )
 
-        late = None
         for side in range(SIDES):
             for c in range(PASSES):
                 by_vector = regroup(c, side * SIDE_TILES, False)
                 by_scalar = regroup(c, side * SIDE_TILES + 1, True)
-                if side > 0 and c == 1:
-                    store_side(side - 1)
-                if late is not None:
-                    quantise_and_multiply(late[0], late[1], late[2])
                 quantise_and_multiply(c, side * SIDE_TILES, by_vector)
-                late = (c, side * SIDE_TILES + 1, by_scalar)
-        quantise_and_multiply(late[0], late[1], late[2])
-        store_side(SIDES - 1)
+                quantise_and_multiply(c, side * SIDE_TILES + 1, by_scalar)
+            store_side(side)

@@ -45,6 +45,7 @@ def tile_builtcontrolled_kernel(tc, state, target_matrix, control, num_qubits, o
         keep = pools.enter_context(tc.tile_pool(name="keep", bufs=1))
         stage = pools.enter_context(tc.tile_pool(name="stage", bufs=GROUPED_BUFS))
         psum = pools.enter_context(tc.psum_pool(name="psum", bufs=PSUM_BANKS))
+        pools.enter_context(tc.manual_schedule())
 
         x_rows = []
         for m in range(ROW_TILES):
@@ -145,10 +146,16 @@ def tile_builtcontrolled_kernel(tc, state, target_matrix, control, num_qubits, o
                         in_=product[:],
                     )
 
+        late = None
         for side in range(SIDES):
             for c in range(PASSES):
                 by_vector = regroup(c, side * SIDE_TILES, False)
                 by_scalar = regroup(c, side * SIDE_TILES + 1, True)
+                if side > 0 and c == 1:
+                    store_side(side - 1)
+                if late is not None:
+                    quantise_and_multiply(late[0], late[1], late[2])
                 quantise_and_multiply(c, side * SIDE_TILES, by_vector)
-                quantise_and_multiply(c, side * SIDE_TILES + 1, by_scalar)
-            store_side(side)
+                late = (c, side * SIDE_TILES + 1, by_scalar)
+        quantise_and_multiply(late[0], late[1], late[2])
+        store_side(SIDES - 1)

@@ -22,9 +22,11 @@ COL_TILES = HALF // N_TILE
 SIDES = 2
 SIDE_COLS = HALF // SIDES
 SIDE_TILES = COL_TILES // SIDES
+ROUNDS = SIDES * PASSES
 PSUM_BANKS = 8
 RUN = 4
 GROUPED_BUFS = 6
+KEPT_AFTER_ROUND = 5
 
 FLOPS = 2 * BATCH * HALF * HALF
 BYTES = 2 * BATCH * DIM + 2 * HALF * HALF + 4 * BATCH * DIM
@@ -47,64 +49,50 @@ def tile_builtcontrolled_kernel(tc, state, target_matrix, control, num_qubits, o
         psum = pools.enter_context(tc.psum_pool(name="psum", bufs=PSUM_BANKS))
         pools.enter_context(tc.manual_schedule())
 
-        x_rows = []
+        w_raw = {}
+
+        def load_round(r):
+            side, c = divmod(r, PASSES)
+            k_rows = target_matrix[HALF + c * K_PASS : HALF + (c + 1) * K_PASS, :]
+            first_tile = side * SIDE_TILES
+            if r == 0:
+                for n in range(first_tile, first_tile + SIDE_TILES):
+                    w_tile = keep.tile([P, PACK, N_TILE], BF16, name="w_raw_%d_%d" % (c, n))
+                    cols = k_rows[:, HALF + n * N_TILE : HALF + (n + 1) * N_TILE]
+                    nc.sync.dma_start(out=w_tile[:], in_=cols.rearrange("(p t) n -> p t n", t=PACK))
+                    w_raw[(c, n)] = w_tile[:]
+            else:
+                w_tile = keep.tile([P, PACK, SIDE_COLS], BF16, name="w_raw_side_%d_%d" % (c, side))
+                cols = k_rows[:, HALF + side * SIDE_COLS : HALF + (side + 1) * SIDE_COLS]
+                nc.sync.dma_start(out=w_tile[:], in_=cols.rearrange("(p t) n -> p t n", t=PACK))
+                for i in range(SIDE_TILES):
+                    w_raw[(c, first_tile + i)] = w_tile[:, :, i * N_TILE : (i + 1) * N_TILE]
+
+        x_on = []
+        x_off = []
         for m in range(ROW_TILES):
-            x_tile = keep.tile([P, DIM], BF16, name="x_rows%d" % m)
-            nc.sync.dma_start(out=x_tile[:], in_=state[m * P : (m + 1) * P, :])
-            x_rows.append(x_tile)
-        w_raw = []
-        for side in range(SIDES):
-            w_raw.append([])
-            for c in range(PASSES):
-                w_tile = keep.tile([P, PACK, SIDE_COLS], BF16, name="w_raw_%d_%d" % (side, c))
-                first_col = HALF + side * SIDE_COLS
-                k_rows = target_matrix[
-                    HALF + c * K_PASS : HALF + (c + 1) * K_PASS, first_col : first_col + SIDE_COLS
-                ]
-                nc.sync.dma_start(out=w_tile[:], in_=k_rows.rearrange("(p t) n -> p t n", t=PACK))
-                w_raw[side].append(w_tile)
+            x_tile = keep.tile([P, HALF], BF16, name="x_on%d" % m)
+            nc.sync.dma_start(out=x_tile[:], in_=state[m * P : (m + 1) * P, HALF:DIM])
+            x_on.append(x_tile)
+        for r in range(ROUNDS):
+            load_round(r)
+            if r == KEPT_AFTER_ROUND:
+                for m in range(ROW_TILES):
+                    x_tile = keep.tile([P, HALF], BF16, name="x_off%d" % m)
+                    nc.sync.dma_start(out=x_tile[:], in_=state[m * P : (m + 1) * P, 0:HALF])
+                    x_off.append(x_tile)
 
         ident = keep.tile([P, P], F32, name="ident")
         make_identity(nc, ident[:])
 
-        x_codes = []
-        x_scales = []
-        for m in range(ROW_TILES):
-            pairs = x_rows[m][:].bitcast(F32).rearrange("r (g p u) -> r g u p", p=P, u=2)
-            x_grouped = keep.tile([P, PASSES * P * PACK], BF16, name="x_grouped%d" % m, align_bytes=64)
-            grouped_pairs = x_grouped[:].bitcast(F32).rearrange("p (c r u) -> p c r u", r=P, u=2)
-            for half in range(2):
-                flipped = psum.tile([P, 2, 2, P], F32, name="flipped", tag="bank")
-                for a in range(2):
-                    c = 2 * half + a
-                    for u in range(2):
-                        nc.tensor.transpose(flipped[:, a, u, :], pairs[:, PASSES + c, u, :], ident[:])
-                copy_on(
-                    nc,
-                    half == 1,
-                    grouped_pairs[:, 2 * half : 2 * half + 2, :, :],
-                    flipped[:].rearrange("p a u r -> p a r u"),
-                )
-            codes = keep.tile([P, PASSES * P], U32, name="x_codes%d" % m, align_bytes=64)
-            scales = keep.tile([P, PASSES * P], U8, name="x_scales%d" % m, align_bytes=64)
-            nc.vector.quantize_mx(out=codes[:].bitcast(FP8X4), scales=scales[:], in_=x_grouped[:])
-            x_codes.append(codes)
-            x_scales.append(scales)
-
-        for m in range(ROW_TILES):
-            kept = keep.tile([P, HALF], F32, name="kept%d" % m)
-            copy_on(nc, m == 0, kept[:], x_rows[m][:, 0:HALF])
-            nc.sync.dma_start(out=out[m * P : (m + 1) * P, 0:HALF], in_=kept[:])
-
-        acc = [
-            [psum.tile([P, N_TILE], F32, name="acc_%d_%d" % (m, n), tag="bank") for n in range(COL_TILES)]
-            for m in range(ROW_TILES)
-        ]
         w_codes = []
         w_scales = []
         for c in range(PASSES):
             w_codes.append(keep.tile([P, HALF], U32, name="w_codes%d" % c, align_bytes=64))
             w_scales.append(keep.tile([P, HALF], U8, name="w_scales%d" % c, align_bytes=64))
+        x_codes = []
+        x_scales = []
+        acc = {}
 
         def regroup(c, n, on_scalar):
             grouped = stage.tile([P, N_TILE, PACK], BF16, name="w_grouped", align_bytes=64)
@@ -112,22 +100,23 @@ def tile_builtcontrolled_kernel(tc, state, target_matrix, control, num_qubits, o
                 nc,
                 on_scalar,
                 grouped[:].rearrange("p (g i) t -> p g t i", i=RUN),
-                w_raw[n // SIDE_TILES][c][
-                    :, :, (n % SIDE_TILES) * N_TILE : (n % SIDE_TILES + 1) * N_TILE
-                ].rearrange("p t (g i) -> p g t i", i=RUN),
+                w_raw[(c, n)].rearrange("p t (g i) -> p g t i", i=RUN),
             )
             return grouped
 
-        def quantise_and_multiply(c, n, grouped):
+        def quantise(c, n, grouped):
             cols = slice(n * N_TILE, (n + 1) * N_TILE)
             nc.vector.quantize_mx(
                 out=w_codes[c][:, cols].bitcast(FP8X4),
                 scales=w_scales[c][:, cols],
                 in_=grouped[:].rearrange("p n t -> p (n t)"),
             )
+
+        def multiply(c, n):
+            cols = slice(n * N_TILE, (n + 1) * N_TILE)
             for m in range(ROW_TILES):
                 nc.tensor.matmul_mx(
-                    out=acc[m][n][:],
+                    out=acc[(m, n)][:],
                     lhsT=x_codes[m][:, c * P : (c + 1) * P].bitcast(FP8X4),
                     lhsT_scale=x_scales[m][:, c * P : (c + 1) * P],
                     rhs=w_codes[c][:, cols].bitcast(FP8X4),
@@ -136,26 +125,75 @@ def tile_builtcontrolled_kernel(tc, state, target_matrix, control, num_qubits, o
                     stop=(c == PASSES - 1),
                 )
 
-        def store_side(side):
-            for n in range(side * SIDE_TILES, (side + 1) * SIDE_TILES):
-                for m in range(ROW_TILES):
-                    product = keep.tile([P, N_TILE], F32, name="product_%d_%d" % (m, n))
-                    copy_on(nc, m == 1, product[:], acc[m][n][:])
-                    nc.sync.dma_start(
-                        out=out[m * P : (m + 1) * P, HALF + n * N_TILE : HALF + (n + 1) * N_TILE],
-                        in_=product[:],
+        def prepare_x():
+            for m in range(ROW_TILES):
+                pairs = x_on[m][:].bitcast(F32).rearrange("r (g p u) -> r g u p", p=P, u=2)
+                x_grouped = keep.tile([P, PASSES * P * PACK], BF16, name="x_grouped%d" % m, align_bytes=64)
+                grouped_pairs = x_grouped[:].bitcast(F32).rearrange("p (c r u) -> p c r u", r=P, u=2)
+                for half in range(2):
+                    flipped = psum.tile([P, 2, 2, P], F32, name="flipped", tag="bank")
+                    for a in range(2):
+                        c = 2 * half + a
+                        for u in range(2):
+                            nc.tensor.transpose(flipped[:, a, u, :], pairs[:, c, u, :], ident[:])
+                    copy_on(
+                        nc,
+                        False,
+                        grouped_pairs[:, 2 * half : 2 * half + 2, :, :],
+                        flipped[:].rearrange("p a u r -> p a r u"),
                     )
+                codes = keep.tile([P, PASSES * P], U32, name="x_codes%d" % m, align_bytes=64)
+                scales = keep.tile([P, PASSES * P], U8, name="x_scales%d" % m, align_bytes=64)
+                nc.vector.quantize_mx(out=codes[:].bitcast(FP8X4), scales=scales[:], in_=x_grouped[:])
+                x_codes.append(codes)
+                x_scales.append(scales)
+
+        def widen(m, on_scalar):
+            kept = keep.tile([P, HALF], F32, name="kept%d" % m)
+            copy_on(nc, on_scalar, kept[:], x_off[m][:])
+            nc.sync.dma_start(out=out[m * P : (m + 1) * P, 0:HALF], in_=kept[:])
+
+        def store_first_side():
+            for m in range(ROW_TILES):
+                product = keep.tile([P, SIDE_COLS], F32, name="product_side%d" % m)
+                for n in range(SIDE_TILES):
+                    copy_on(nc, True, product[:, n * N_TILE : (n + 1) * N_TILE], acc[(m, n)][:])
+                nc.sync.dma_start(out=out[m * P : (m + 1) * P, HALF : HALF + SIDE_COLS], in_=product[:])
+
+        def store_bank(m, n, on_scalar):
+            product = keep.tile([P, N_TILE], F32, name="product_%d_%d" % (m, n))
+            copy_on(nc, on_scalar, product[:], acc[(m, n)][:])
+            nc.sync.dma_start(
+                out=out[m * P : (m + 1) * P, HALF + n * N_TILE : HALF + (n + 1) * N_TILE], in_=product[:]
+            )
+
+        prepare_x()
+        for n in range(COL_TILES):
+            for m in range(ROW_TILES):
+                acc[(m, n)] = psum.tile([P, N_TILE], F32, name="acc_%d_%d" % (m, n), tag="bank")
 
         late = None
-        for side in range(SIDES):
-            for c in range(PASSES):
-                by_vector = regroup(c, side * SIDE_TILES, False)
-                by_scalar = regroup(c, side * SIDE_TILES + 1, True)
-                if side > 0 and c == 1:
-                    store_side(side - 1)
-                if late is not None:
-                    quantise_and_multiply(late[0], late[1], late[2])
-                quantise_and_multiply(c, side * SIDE_TILES, by_vector)
-                late = (c, side * SIDE_TILES + 1, by_scalar)
-        quantise_and_multiply(late[0], late[1], late[2])
-        store_side(SIDES - 1)
+        for r in range(ROUNDS):
+            side, c = divmod(r, PASSES)
+            n_scalar = side * SIDE_TILES
+            n_vector = n_scalar + 1
+            by_scalar = regroup(c, n_scalar, True)
+            by_vector = regroup(c, n_vector, False)
+            if r == KEPT_AFTER_ROUND:
+                store_first_side()
+                widen(0, True)
+                widen(1, False)
+            if late is not None:
+                quantise(late[0], late[1], late[2])
+                multiply(late[0], late[1])
+            quantise(c, n_vector, by_vector)
+            multiply(c, n_vector)
+            late = (c, n_scalar, by_scalar)
+        last_vector = COL_TILES - 1
+        last_scalar = COL_TILES - 2
+        quantise(late[0], late[1], late[2])
+        store_bank(0, last_vector, True)
+        store_bank(1, last_vector, True)
+        multiply(late[0], late[1])
+        store_bank(0, last_scalar, True)
+        store_bank(1, last_scalar, False)

@@ -181,7 +181,7 @@ def tile_builtcontrolled_kernel(tc, state, target_matrix, control, num_qubits, o
             by_vector = regroup(c, n_vector, False)
             if r == KEPT_AFTER_ROUND:
                 store_first_side()
-                widen(0, True)
+                widen(0, False)
                 widen(1, False)
             if late is not None:
                 quantise(late[0], late[1], late[2])

@@ -55,18 +55,11 @@ def tile_builtcontrolled_kernel(tc, state, target_matrix, control, num_qubits, o
             side, c = divmod(r, PASSES)
             k_rows = target_matrix[HALF + c * K_PASS : HALF + (c + 1) * K_PASS, :]
             first_tile = side * SIDE_TILES
-            if r == 0:
-                for n in range(first_tile, first_tile + SIDE_TILES):
-                    w_tile = keep.tile([P, PACK, N_TILE], BF16, name="w_raw_%d_%d" % (c, n))
-                    cols = k_rows[:, HALF + n * N_TILE : HALF + (n + 1) * N_TILE]
-                    nc.sync.dma_start(out=w_tile[:], in_=cols.rearrange("(p t) n -> p t n", t=PACK))
-                    w_raw[(c, n)] = w_tile[:]
-            else:
-                w_tile = keep.tile([P, PACK, SIDE_COLS], BF16, name="w_raw_side_%d_%d" % (c, side))
-                cols = k_rows[:, HALF + side * SIDE_COLS : HALF + (side + 1) * SIDE_COLS]
-                nc.sync.dma_start(out=w_tile[:], in_=cols.rearrange("(p t) n -> p t n", t=PACK))
-                for i in range(SIDE_TILES):
-                    w_raw[(c, first_tile + i)] = w_tile[:, :, i * N_TILE : (i + 1) * N_TILE]
+            w_tile = keep.tile([P, PACK, SIDE_COLS], BF16, name="w_raw_side_%d_%d" % (c, side))
+            cols = k_rows[:, HALF + side * SIDE_COLS : HALF + (side + 1) * SIDE_COLS]
+            nc.sync.dma_start(out=w_tile[:], in_=cols.rearrange("(p t) n -> p t n", t=PACK))
+            for i in range(SIDE_TILES):
+                w_raw[(c, first_tile + i)] = w_tile[:, :, i * N_TILE : (i + 1) * N_TILE]
 
         x_on = []
         x_off = []
@@ -148,24 +141,21 @@ def tile_builtcontrolled_kernel(tc, state, target_matrix, control, num_qubits, o
                 x_codes.append(codes)
                 x_scales.append(scales)
 
+        out_left = [keep.tile([P, HALF + SIDE_COLS], F32, name="out_left%d" % m) for m in range(ROW_TILES)]
+        out_right = [keep.tile([P, SIDE_COLS], F32, name="out_right%d" % m) for m in range(ROW_TILES)]
+
         def widen(m, on_scalar):
-            kept = keep.tile([P, HALF], F32, name="kept%d" % m)
-            copy_on(nc, on_scalar, kept[:], x_off[m][:])
-            nc.sync.dma_start(out=out[m * P : (m + 1) * P, 0:HALF], in_=kept[:])
+            copy_on(nc, on_scalar, out_left[m][:, 0:HALF], x_off[m][:])
 
-        def store_first_side():
+        def store_left():
             for m in range(ROW_TILES):
-                product = keep.tile([P, SIDE_COLS], F32, name="product_side%d" % m)
                 for n in range(SIDE_TILES):
-                    copy_on(nc, True, product[:, n * N_TILE : (n + 1) * N_TILE], acc[(m, n)][:])
-                nc.sync.dma_start(out=out[m * P : (m + 1) * P, HALF : HALF + SIDE_COLS], in_=product[:])
+                    copy_on(nc, True, out_left[m][:, HALF + n * N_TILE : HALF + (n + 1) * N_TILE], acc[(m, n)][:])
+                nc.sync.dma_start(out=out[m * P : (m + 1) * P, 0 : HALF + SIDE_COLS], in_=out_left[m][:])
 
-        def store_bank(m, n, on_scalar):
-            product = keep.tile([P, N_TILE], F32, name="product_%d_%d" % (m, n))
-            copy_on(nc, on_scalar, product[:], acc[(m, n)][:])
-            nc.sync.dma_start(
-                out=out[m * P : (m + 1) * P, HALF + n * N_TILE : HALF + (n + 1) * N_TILE], in_=product[:]
-            )
+        def empty_bank(m, n, on_scalar):
+            i = n - SIDE_TILES
+            copy_on(nc, on_scalar, out_right[m][:, i * N_TILE : (i + 1) * N_TILE], acc[(m, n)][:])
 
         prepare_x()
         for n in range(COL_TILES):
@@ -180,9 +170,9 @@ def tile_builtcontrolled_kernel(tc, state, target_matrix, control, num_qubits, o
             by_scalar = regroup(c, n_scalar, True)
             by_vector = regroup(c, n_vector, False)
             if r == KEPT_AFTER_ROUND:
-                store_first_side()
                 widen(0, False)
                 widen(1, False)
+                store_left()
             if late is not None:
                 quantise(late[0], late[1], late[2])
                 multiply(late[0], late[1])
@@ -192,8 +182,10 @@ def tile_builtcontrolled_kernel(tc, state, target_matrix, control, num_qubits, o
         last_vector = COL_TILES - 1
         last_scalar = COL_TILES - 2
         quantise(late[0], late[1], late[2])
-        store_bank(0, last_vector, True)
-        store_bank(1, last_vector, True)
+        empty_bank(0, last_vector, True)
+        empty_bank(1, last_vector, False)
         multiply(late[0], late[1])
-        store_bank(0, last_scalar, True)
-        store_bank(1, last_scalar, False)
+        empty_bank(0, last_scalar, True)
+        empty_bank(1, last_scalar, False)
+        for m in range(ROW_TILES):
+            nc.sync.dma_start(out=out[m * P : (m + 1) * P, HALF + SIDE_COLS : DIM], in_=out_right[m][:])

from contextlib import ExitStack

import concourse.mybir as mybir
from concourse.masks import make_identity

BF16 = mybir.dt.bfloat16
F32 = mybir.dt.float32
U32 = mybir.dt.uint32
U8 = mybir.dt.uint8
FP8X4 = mybir.dt.float8_e4m3fn_x4

P = 128
PACK = 4
K_PASS = P * PACK
BATCH = 256
DIM = 4096
HALF = DIM // 2
ROW_TILES = BATCH // P
PASSES = HALF // K_PASS
N_TILE = 512
COL_TILES = HALF // N_TILE
SIDES = 2
SIDE_COLS = HALF // SIDES
SIDE_TILES = COL_TILES // SIDES
ROUNDS = SIDES * PASSES
PSUM_BANKS = 8
RUN = 4
GROUPED_BUFS = 6
KEPT_AFTER_ROUND = 5

FLOPS = 2 * BATCH * HALF * HALF
BYTES = 2 * BATCH * DIM + 2 * HALF * HALF + 4 * BATCH * DIM


def copy_on(nc, on_scalar, out, in_):
    if on_scalar:
        nc.scalar.copy(out=out, in_=in_)
    else:
        nc.vector.tensor_copy(out=out, in_=in_)


def tile_builtcontrolled_kernel(tc, state, target_matrix, control, num_qubits, out):
    nc = tc.nc
    assert control == 0 and num_qubits == 12

    with ExitStack() as pools:
        keep = pools.enter_context(tc.tile_pool(name="keep", bufs=1))
        stage = pools.enter_context(tc.tile_pool(name="stage", bufs=GROUPED_BUFS))
        psum = pools.enter_context(tc.psum_pool(name="psum", bufs=PSUM_BANKS))
        pools.enter_context(tc.manual_schedule())

        w_raw = {}

        def load_round(r):
            side, c = divmod(r, PASSES)
            k_rows = target_matrix[HALF + c * K_PASS : HALF + (c + 1) * K_PASS, :]
            first_tile = side * SIDE_TILES
            w_tile = keep.tile([P, PACK, SIDE_COLS], BF16, name="w_raw_side_%d_%d" % (c, side))
            cols = k_rows[:, HALF + side * SIDE_COLS : HALF + (side + 1) * SIDE_COLS]
            nc.sync.dma_start(out=w_tile[:], in_=cols.rearrange("(p t) n -> p t n", t=PACK))
            for i in range(SIDE_TILES):
                w_raw[(c, first_tile + i)] = w_tile[:, :, i * N_TILE : (i + 1) * N_TILE]

        x_on = []
        x_off = []
        for m in range(ROW_TILES):
            x_tile = keep.tile([P, HALF], BF16, name="x_on%d" % m)
            nc.sync.dma_start(out=x_tile[:], in_=state[m * P : (m + 1) * P, HALF:DIM])
            x_on.append(x_tile)
        for r in range(ROUNDS):
            load_round(r)
            if r == KEPT_AFTER_ROUND:
                for m in range(ROW_TILES):
                    x_tile = keep.tile([P, HALF], BF16, name="x_off%d" % m)
                    nc.sync.dma_start(out=x_tile[:], in_=state[m * P : (m + 1) * P, 0:HALF])
                    x_off.append(x_tile)

        ident = keep.tile([P, P], F32, name="ident")
        make_identity(nc, ident[:])

        w_codes = []
        w_scales = []
        for c in range(PASSES):
            w_codes.append(keep.tile([P, HALF], U32, name="w_codes%d" % c, align_bytes=64))
            w_scales.append(keep.tile([P, HALF], U8, name="w_scales%d" % c, align_bytes=64))
        x_codes = []
        x_scales = []
        acc = {}

        def regroup(c, n, on_scalar):
            grouped = stage.tile([P, N_TILE, PACK], BF16, name="w_grouped", align_bytes=64)
            copy_on(
                nc,
                on_scalar,
                grouped[:].rearrange("p (g i) t -> p g t i", i=RUN),
                w_raw[(c, n)].rearrange("p t (g i) -> p g t i", i=RUN),
            )
            return grouped

        def quantise(c, n, grouped):
            cols = slice(n * N_TILE, (n + 1) * N_TILE)
            nc.vector.quantize_mx(
                out=w_codes[c][:, cols].bitcast(FP8X4),
                scales=w_scales[c][:, cols],
                in_=grouped[:].rearrange("p n t -> p (n t)"),
            )

        def multiply(c, n):
            cols = slice(n * N_TILE, (n + 1) * N_TILE)
            for m in range(ROW_TILES):
                nc.tensor.matmul_mx(
                    out=acc[(m, n)][:],
                    lhsT=x_codes[m][:, c * P : (c + 1) * P].bitcast(FP8X4),
                    lhsT_scale=x_scales[m][:, c * P : (c + 1) * P],
                    rhs=w_codes[c][:, cols].bitcast(FP8X4),
                    rhs_scale=w_scales[c][:, cols],
                    start=(c == 0),
                    stop=(c == PASSES - 1),
                )

        def prepare_x():
            for m in range(ROW_TILES):
                pairs = x_on[m][:].bitcast(F32).rearrange("r (g p u) -> r g u p", p=P, u=2)
                x_grouped = keep.tile([P, PASSES * P * PACK], BF16, name="x_grouped%d" % m, align_bytes=64)
                grouped_pairs = x_grouped[:].bitcast(F32).rearrange("p (c r u) -> p c r u", r=P, u=2)
                for half in range(2):
                    flipped = psum.tile([P, 2, 2, P], F32, name="flipped", tag="bank")
                    for a in range(2):
                        c = 2 * half + a
                        for u in range(2):
                            nc.tensor.transpose(flipped[:, a, u, :], pairs[:, c, u, :], ident[:])
                    copy_on(
                        nc,
                        False,
                        grouped_pairs[:, 2 * half : 2 * half + 2, :, :],
                        flipped[:].rearrange("p a u r -> p a r u"),
                    )
                codes = keep.tile([P, PASSES * P], U32, name="x_codes%d" % m, align_bytes=64)
                scales = keep.tile([P, PASSES * P], U8, name="x_scales%d" % m, align_bytes=64)
                nc.vector.quantize_mx(out=codes[:].bitcast(FP8X4), scales=scales[:], in_=x_grouped[:])
                x_codes.append(codes)
                x_scales.append(scales)

        out_left = [keep.tile([P, HALF + SIDE_COLS], F32, name="out_left%d" % m) for m in range(ROW_TILES)]
        out_right = [keep.tile([P, SIDE_COLS], F32, name="out_right%d" % m) for m in range(ROW_TILES)]

        def widen(m, on_scalar):
            copy_on(nc, on_scalar, out_left[m][:, 0:HALF], x_off[m][:])

        def store_left():
            for m in range(ROW_TILES):
                for n in range(SIDE_TILES):
                    copy_on(nc, True, out_left[m][:, HALF + n * N_TILE : HALF + (n + 1) * N_TILE], acc[(m, n)][:])
                nc.sync.dma_start(out=out[m * P : (m + 1) * P, 0 : HALF + SIDE_COLS], in_=out_left[m][:])

        def empty_bank(m, n, on_scalar):
            i = n - SIDE_TILES
            copy_on(nc, on_scalar, out_right[m][:, i * N_TILE : (i + 1) * N_TILE], acc[(m, n)][:])

        prepare_x()
        for n in range(COL_TILES):
            for m in range(ROW_TILES):
                acc[(m, n)] = psum.tile([P, N_TILE], F32, name="acc_%d_%d" % (m, n), tag="bank")

        late = None
        for r in range(ROUNDS):
            side, c = divmod(r, PASSES)
            n_scalar = side * SIDE_TILES
            n_vector = n_scalar + 1
            by_scalar = regroup(c, n_scalar, True)
            by_vector = regroup(c, n_vector, False)
            if r == KEPT_AFTER_ROUND:
                widen(0, False)
                widen(1, False)
                store_left()
            if late is not None:
                quantise(late[0], late[1], late[2])
                multiply(late[0], late[1])
            quantise(c, n_vector, by_vector)
            multiply(c, n_vector)
            late = (c, n_scalar, by_scalar)
        last_vector = COL_TILES - 1
        last_scalar = COL_TILES - 2
        quantise(late[0], late[1], late[2])
        empty_bank(0, last_vector, True)
        empty_bank(1, last_vector, False)
        multiply(late[0], late[1])
        empty_bank(0, last_scalar, True)
        empty_bank(1, last_scalar, False)
        for m in range(ROW_TILES):
            nc.sync.dma_start(out=out[m * P : (m + 1) * P, HALF + SIDE_COLS : DIM], in_=out_right[m][:])
